import numpy as np
import ml_dtypes


def mxq(x, axis, fmt="e4m3"):
    dtype, down = {"e4m3": (ml_dtypes.float8_e4m3fn, 7), "e5m2": (ml_dtypes.float8_e5m2, 14)}[fmt]
    v = np.moveaxis(np.asarray(x, np.float32).astype(ml_dtypes.bfloat16).astype(np.float64), axis, -1)
    blocks = v.reshape(v.shape[:-1] + (-1, 32))
    amax = np.abs(blocks).max(-1, keepdims=True)
    byte = np.maximum(np.where(amax > 0, np.frexp(amax)[1] - 1 + 127, 0) - down, 1)
    scale = np.exp2(byte - 127.0)
    codes = (blocks / scale).astype(np.float32).astype(dtype).astype(np.float64)
    return np.moveaxis((codes * scale).reshape(v.shape), -1, axis)


WIDE = False


def mx_kscale(k):
    if not WIDE:
        return np.ones(k)
    levels = np.array([10, -10, 5, -5, 0])
    a = np.random.permutation(np.resize(levels, k // 512 * 4)).reshape(k // 512, 4)
    idx = np.arange(k)
    return np.exp2(a[idx // 512, idx % 128 // 32])


BF16 = ml_dtypes.bfloat16


def bf(x):
    return np.asarray(x, np.float32).astype(BF16)


def f64(x):
    return np.asarray(x).astype(np.float64)


B, G, C0, C1, C2, NO = 2, 32, 8192, 512, 1024, 128
G0, G1, G2 = G, G // 2, G // 4
STRIDES = (8.0, 16.0, 32.0)


def sigmoid(v):
    return 1.0 / (1.0 + np.exp(-v))


def decode_level(feat, W, b, stride, level):
    bs, _, ny, nx = feat.shape
    p = (mxq(feat, 1, "e4m3").transpose(0, 2, 3, 1) @ mxq(W, 1, "e4m3").T) + b
    y = sigmoid(p)
    xv = np.arange(nx, dtype=np.float64)
    yv = np.arange(ny, dtype=np.float64)[:, None]
    power = 2.0 ** level
    d = (y[..., :4] * 2.0) ** 2 * power
    x1 = (xv + 1.0 - d[..., 0]) * stride
    y1 = (yv + 1.0 - d[..., 1]) * stride
    x2 = (xv + d[..., 2]) * stride
    y2 = (yv + d[..., 3]) * stride
    box = np.stack([(x1 + x2) * 0.5, (y1 + y2) * 0.5, x2 - x1, y2 - y1], axis=-1)
    out = np.concatenate([box, y[..., 4:]], axis=-1)
    return out.reshape(bs, ny * nx, out.shape[-1])


def setup_inputs():
    s0, s1, s2 = mx_kscale(C0), mx_kscale(C1), mx_kscale(C2)
    return {
        "x0": bf(np.random.standard_normal((B, C0, G0, G0)) * s0[None, :, None, None]),
        "x1": bf(np.random.standard_normal((B, C1, G1, G1)) * s1[None, :, None, None]),
        "x2": bf(np.random.standard_normal((B, C2, G2, G2)) * s2[None, :, None, None]),
        "W0": bf(np.random.standard_normal((NO, C0)) / np.sqrt(C0) / s0),
        "b0": bf(np.random.standard_normal(NO) * 0.5),
        "W1": bf(np.random.standard_normal((NO, C1)) / np.sqrt(C1) / s1),
        "b1": bf(np.random.standard_normal(NO) * 0.5),
        "W2": bf(np.random.standard_normal((NO, C2)) / np.sqrt(C2) / s2),
        "b2": bf(np.random.standard_normal(NO) * 0.5),
    }


def reference(x0, x1, x2, W0, b0, W1, b1, W2, b2):
    feats = (f64(x0), f64(x1), f64(x2))
    Ws = (f64(W0), f64(W1), f64(W2))
    bs_ = (f64(b0), f64(b1), f64(b2))
    z = [decode_level(feats[i], Ws[i], bs_[i], STRIDES[i], i) for i in range(3)]
    return np.concatenate(z, axis=1)

@@ -1,0 +1,229 @@
+from contextlib import ExitStack
+
+import concourse.mybir as mybir
+from concourse.masks import make_identity
+
+BF16 = mybir.dt.bfloat16
+F32 = mybir.dt.float32
+I32 = mybir.dt.int32
+U32 = mybir.dt.uint32
+U8 = mybir.dt.uint8
+FP8X4 = mybir.dt.float8_e4m3fn_x4
+ACT = mybir.ActivationFunctionType
+ALU = mybir.AluOpType
+
+P = 128
+PACK = 4
+K_PASS = P * PACK
+BANK = 512
+B = 2
+NO = 128
+RUN = 4
+
+CHANNELS = (8192, 512, 1024)
+SIDE = (32, 16, 8)
+SIDE_BITS = (5, 4, 3)
+STRIDE = (8.0, 16.0, 32.0)
+POWER = (1.0, 2.0, 4.0)
+FIRST_ROW = (0, 1024, 1280)
+
+CELLS0 = SIDE[0] * SIDE[0]
+PASSES0 = CHANNELS[0] // K_PASS
+VECTOR_CELLS = 512
+
+FLOPS = 2 * NO * B * (8192 * 32 * 32 + 512 * 16 * 16 + 1024 * 8 * 8)
+
+
+def regroup(copy, grouped, raw):
+    copy(
+        out=grouped.rearrange("p (c i) j -> p c j i", i=RUN),
+        in_=raw.rearrange("p j (c i) -> p c j i", i=RUN),
+    )
+
+
+def tile_objectboxdetect_k_kernel(tc, x0, x1, x2, W0, b0, W1, b1, W2, b2, out):
+    nc = tc.nc
+    weights = (W0, W1, W2)
+    biases = (b0, b1, b2)
+
+    with ExitStack() as ctx:
+        keep = ctx.enter_context(tc.tile_pool(name="keep", bufs=1))
+        raw_pool = ctx.enter_context(tc.tile_pool(name="raw", bufs=8))
+        work = ctx.enter_context(tc.tile_pool(name="work", bufs=3))
+        acc_pool = ctx.enter_context(tc.psum_pool(name="acc", bufs=4))
+        turn_pool = ctx.enter_context(tc.psum_pool(name="turn", bufs=4))
+
+        ident = keep.tile([P, P], F32, name="ident")
+        make_identity(nc, ident[:])
+
+        warm = keep.tile([P, 1], F32, name="warm")
+        nc.vector.memset(warm[:], 0.0)
+        nc.scalar.activation(out=warm[:], in_=warm[:], func=ACT.Sigmoid)
+
+        bias_sb = []
+        for level in range(3):
+            bias = keep.tile([P, 1], BF16, name="bias%d" % level)
+            nc.scalar.dma_start(out=bias[:], in_=biases[level].rearrange("(o one) -> o one", one=1))
+            bias_sb.append(bias)
+
+        def make_grid(level, banks, per_part):
+            side = SIDE[level]
+            cell = keep.tile([P, banks, per_part], I32, name="cell%d" % level)
+            nc.gpsimd.iota(cell[:], pattern=[[BANK, banks], [1, per_part]], base=0, channel_multiplier=per_part)
+            col = keep.tile([P, banks, per_part], I32, name="col%d" % level)
+            nc.vector.tensor_scalar(out=col[:], in0=cell[:], scalar1=side - 1, scalar2=None, op0=ALU.bitwise_and)
+            row = keep.tile([P, banks, per_part], I32, name="row%d" % level)
+            nc.vector.tensor_scalar(
+                out=row[:], in0=cell[:], scalar1=side * side - 1, scalar2=SIDE_BITS[level],
+                op0=ALU.bitwise_and, op1=ALU.logical_shift_right,
+            )
+            grid = keep.tile([P, banks, per_part, 2], F32, name="grid%d" % level)
+            for axis, index in enumerate((col, row)):
+                nc.vector.tensor_scalar(
+                    out=grid[:, :, :, axis], in0=index[:], scalar1=0.5, scalar2=STRIDE[level],
+                    op0=ALU.add, op1=ALU.mult,
+                )
+            return grid
+
+        grids = (make_grid(0, 2, 4), make_grid(1, 1, 4), make_grid(2, 1, 1))
+
+        def load_weights(level):
+            w_raw = keep.tile([P, CHANNELS[level]], BF16, name="w_raw%d" % level)
+            piece = min(CHANNELS[level], 4 * K_PASS)
+            for first in range(0, CHANNELS[level], piece):
+                nc.sync.dma_start(out=w_raw[:, first : first + piece], in_=weights[level][:, first : first + piece])
+            return w_raw
+
+        def quantise_weights(level, w_raw):
+            passes = CHANNELS[level] // K_PASS
+            w_codes = keep.tile([P, passes, NO], U32, name="w_codes%d" % level, align_bytes=64)
+            w_scales = keep.tile([P, passes, NO], U8, name="w_scales%d" % level, align_bytes=64)
+            w_words = w_raw[:].bitcast(F32)
+            words = K_PASS // 2
+            for g0 in range(0, passes, 2):
+                count = min(2, passes - g0)
+                planes = turn_pool.tile([P, count, 2, NO], F32, name="planes", tag="turn")
+                for j in range(count):
+                    for u in range(2):
+                        first = (g0 + j) * words + u
+                        nc.tensor.transpose(planes[:, j, u, :], w_words[:, first : (g0 + j + 1) * words : 2], ident[:])
+                w_grouped = work.tile([P, count, NO, PACK], BF16, name="w_grouped", tag="w_grouped", align_bytes=64)
+                copy = nc.vector.tensor_copy if (g0 // 2) % 2 == 0 else nc.scalar.copy
+                copy(out=w_grouped[:].bitcast(F32), in_=planes[:].rearrange("p j u o -> p j o u"))
+                nc.vector.quantize_mx(
+                    out=w_codes[:, g0 : g0 + count, :].rearrange("p g o -> p (g o)").bitcast(FP8X4),
+                    scales=w_scales[:, g0 : g0 + count, :].rearrange("p g o -> p (g o)"),
+                    in_=w_grouped[:].rearrange("p g o t -> p (g o t)"),
+                )
+            return w_codes, w_scales
+
+        def finish(level, acc, per_part, grid, stores):
+            y = work.tile([P, per_part, P], F32, name="y", tag="y")
+            nc.scalar.activation(
+                out=y[:], in_=acc.rearrange("o (p t) -> o t p", t=per_part), func=ACT.Sigmoid,
+                bias=bias_sb[level][:, 0:1], scale=1.0,
+            )
+            turned = turn_pool.tile([P, per_part, NO], F32, name="turned", tag="turn")
+            for t in range(per_part):
+                nc.tensor.transpose(turned[:, t, :], y[:, t, :], ident[:])
+            res = work.tile([P, per_part, NO], F32, name="res", tag="res")
+            nc.vector.tensor_copy(out=res[:], in_=turned[:])
+            stride, power = STRIDE[level], POWER[level]
+            sq = work.tile([P, per_part, 4], F32, name="sq", tag="sq")
+            nc.vector.tensor_tensor(out=sq[:], in0=res[:, :, 0:4], in1=res[:, :, 0:4], op=ALU.mult)
+            diff = work.tile([P, per_part, 2], F32, name="diff", tag="diff")
+            nc.vector.tensor_tensor(out=diff[:], in0=sq[:, :, 2:4], in1=sq[:, :, 0:2], op=ALU.subtract)
+            total = work.tile([P, per_part, 2], F32, name="total", tag="total")
+            nc.vector.tensor_tensor(out=total[:], in0=sq[:, :, 2:4], in1=sq[:, :, 0:2], op=ALU.add)
+            nc.vector.scalar_tensor_tensor(
+                out=res[:, :, 0:2], in0=diff[:], scalar=2.0 * stride * power, in1=grid,
+                op0=ALU.mult, op1=ALU.add,
+            )
+            nc.vector.tensor_scalar(
+                out=res[:, :, 2:4], in0=total[:], scalar1=4.0 * stride * power, scalar2=-stride,
+                op0=ALU.mult, op1=ALU.add,
+            )
+            for rows, parts in stores:
+                nc.sync.dma_start(out=rows.rearrange("(p t) o -> p t o", t=per_part), in_=res[parts, :, :])
+
+        def small_level(level, x):
+            passes = CHANNELS[level] // K_PASS
+            cells = SIDE[level] * SIDE[level]
+            w_raw = load_weights(level)
+            raw = keep.tile([P, B, passes, PACK, cells], BF16, name="raw%d" % level)
+            nc.sync.dma_start(
+                out=raw[:].rearrange("p n g j w -> p (n g) (j w)"),
+                in_=x.rearrange("n (g p j) r c -> p (n g) (j r c)", p=P, j=PACK),
+            )
+            w_codes, w_scales = quantise_weights(level, w_raw)
+            grouped = keep.tile([P, passes, B, cells, PACK], BF16, name="grouped%d" % level, align_bytes=64)
+            for n in range(B):
+                copy = nc.vector.tensor_copy if n == 0 else nc.scalar.copy
+                for g in range(passes):
+                    regroup(copy, grouped[:, g, n, :, :], raw[:, n, g, :, :])
+            codes = keep.tile([P, passes, B * cells], U32, name="codes%d" % level, align_bytes=64)
+            scales = keep.tile([P, passes, B * cells], U8, name="scales%d" % level, align_bytes=64)
+            nc.vector.quantize_mx(
+                out=codes[:].rearrange("p g w -> p (g w)").bitcast(FP8X4),
+                scales=scales[:].rearrange("p g w -> p (g w)"),
+                in_=grouped[:].rearrange("p g n w j -> p (g n w j)"),
+            )
+            acc = acc_pool.tile([P, B * cells], F32, name="acc", tag="acc")
+            for g in range(passes):
+                nc.tensor.matmul_mx(
+                    out=acc[:],
+                    lhsT=w_codes[:, g, :].bitcast(FP8X4), lhsT_scale=w_scales[:, g, :],
+                    rhs=codes[:, g, :].bitcast(FP8X4), rhs_scale=scales[:, g, :],
+                    start=(g == 0), stop=(g == passes - 1),
+                )
+            half = P // B
+            first = FIRST_ROW[level]
+            finish(
+                level, acc[:], B * cells // P, grids[level][:, 0, :, :],
+                [(out[n, first : first + cells, :], slice(n * half, (n + 1) * half)) for n in range(B)],
+            )
+
+        small_level(2, x2)
+        small_level(1, x1)
+
+        w_codes0, w_scales0 = quantise_weights(0, load_weights(0))
+
+        def load_and_regroup(n, c):
+            raw = raw_pool.tile([P, PACK, CELLS0], BF16, name="raw")
+            nc.sync.dma_start(
+                out=raw[:],
+                in_=x0[n, c * K_PASS : (c + 1) * K_PASS, :, :].rearrange("(p j) r c -> p j (r c)", j=PACK),
+            )
+            grouped = work.tile([P, CELLS0, PACK], BF16, name="grouped", tag="grouped", align_bytes=64)
+            regroup(nc.vector.tensor_copy, grouped[:, :VECTOR_CELLS, :], raw[:, :, :VECTOR_CELLS])
+            regroup(nc.scalar.copy, grouped[:, VECTOR_CELLS:, :], raw[:, :, VECTOR_CELLS:])
+            return grouped
+
+        chunks = [(n, c) for n in range(B) for c in range(PASSES0)]
+        grouped_next = load_and_regroup(*chunks[0])
+        acc = None
+        for i, (n, c) in enumerate(chunks):
+            grouped = grouped_next
+            if i + 1 < len(chunks):
+                grouped_next = load_and_regroup(*chunks[i + 1])
+            codes = work.tile([P, CELLS0], U32, name="codes", tag="codes", align_bytes=64)
+            scales = work.tile([P, CELLS0], U8, name="scales", tag="scales", align_bytes=64)
+            nc.vector.quantize_mx(
+                out=codes[:].bitcast(FP8X4), scales=scales[:], in_=grouped[:].rearrange("p w j -> p (w j)"),
+            )
+            if c == 0:
+                acc = [acc_pool.tile([P, BANK], F32, name="acc%d" % h, tag="acc") for h in range(CELLS0 // BANK)]
+            for h in range(CELLS0 // BANK):
+                cols = slice(h * BANK, (h + 1) * BANK)
+                nc.tensor.matmul_mx(
+                    out=acc[h][:],
+                    lhsT=w_codes0[:, c, :].bitcast(FP8X4), lhsT_scale=w_scales0[:, c, :],
+                    rhs=codes[:, cols].bitcast(FP8X4), rhs_scale=scales[:, cols],
+                    start=(c == 0), stop=(c == PASSES0 - 1),
+                )
+            if c == PASSES0 - 1:
+                for h in range(CELLS0 // BANK):
+                    finish(
+                        0, acc[h][:], BANK // P, grids[0][:, h, :, :],
+                        [(out[n, h * BANK : (h + 1) * BANK, :], slice(0, P))],
+                    )

@@ -28,6 +28,7 @@ POWER = (1.0, 2.0, 4.0)
 FIRST_ROW = (0, 1024, 1280)
 
 CELLS0 = SIDE[0] * SIDE[0]
+BANKS0 = CELLS0 // BANK
 PASSES0 = CHANNELS[0] // K_PASS
 VECTOR_CELLS = 512
 
@@ -43,15 +44,44 @@ def regroup(copy, grouped, raw):
 
 def tile_objectboxdetect_k_kernel(tc, x0, x1, x2, W0, b0, W1, b1, W2, b2, out):
     nc = tc.nc
+    features = (x0, x1, x2)
     weights = (W0, W1, W2)
     biases = (b0, b1, b2)
 
     with ExitStack() as ctx:
+        ctx.enter_context(tc.manual_schedule())
         keep = ctx.enter_context(tc.tile_pool(name="keep", bufs=1))
         raw_pool = ctx.enter_context(tc.tile_pool(name="raw", bufs=8))
         work = ctx.enter_context(tc.tile_pool(name="work", bufs=3))
         acc_pool = ctx.enter_context(tc.psum_pool(name="acc", bufs=4))
         turn_pool = ctx.enter_context(tc.psum_pool(name="turn", bufs=4))
+
+        bias_sb = []
+        for level in range(3):
+            bias = keep.tile([P, 1], BF16, name="bias%d" % level)
+            nc.scalar.dma_start(out=bias[:], in_=biases[level].rearrange("(o one) -> o one", one=1))
+            bias_sb.append(bias)
+
+        def load_weights(level):
+            w_raw = keep.tile([P, CHANNELS[level]], BF16, name="w_raw%d" % level)
+            piece = min(CHANNELS[level], 4 * K_PASS)
+            for first in range(0, CHANNELS[level], piece):
+                nc.sync.dma_start(out=w_raw[:, first : first + piece], in_=weights[level][:, first : first + piece])
+            return w_raw
+
+        def load_small(level):
+            raw = keep.tile(
+                [P, B, CHANNELS[level] // K_PASS, PACK, SIDE[level] * SIDE[level]], BF16, name="raw%d" % level
+            )
+            nc.sync.dma_start(
+                out=raw[:].rearrange("p n g j w -> p (n g) (j w)"),
+                in_=features[level].rearrange("n (g p j) r c -> p (n g) (j r c)", p=P, j=PACK),
+            )
+            return raw
+
+        w_raw2, w_raw1 = load_weights(2), load_weights(1)
+        raw2, raw1 = load_small(2), load_small(1)
+        w_raw0 = load_weights(0)
 
         ident = keep.tile([P, P], F32, name="ident")
         make_identity(nc, ident[:])
@@ -59,12 +89,6 @@ def tile_objectboxdetect_k_kernel(tc, x0, x1, x2, W0, b0, W1, b1, W2, b2, out):
         warm = keep.tile([P, 1], F32, name="warm")
         nc.vector.memset(warm[:], 0.0)
         nc.scalar.activation(out=warm[:], in_=warm[:], func=ACT.Sigmoid)
-
-        bias_sb = []
-        for level in range(3):
-            bias = keep.tile([P, 1], BF16, name="bias%d" % level)
-            nc.scalar.dma_start(out=bias[:], in_=biases[level].rearrange("(o one) -> o one", one=1))
-            bias_sb.append(bias)
 
         def make_grid(level, banks, per_part):
             side = SIDE[level]
@@ -85,14 +109,7 @@ def tile_objectboxdetect_k_kernel(tc, x0, x1, x2, W0, b0, W1, b1, W2, b2, out):
                 )
             return grid
 
-        grids = (make_grid(0, 2, 4), make_grid(1, 1, 4), make_grid(2, 1, 1))
-
-        def load_weights(level):
-            w_raw = keep.tile([P, CHANNELS[level]], BF16, name="w_raw%d" % level)
-            piece = min(CHANNELS[level], 4 * K_PASS)
-            for first in range(0, CHANNELS[level], piece):
-                nc.sync.dma_start(out=w_raw[:, first : first + piece], in_=weights[level][:, first : first + piece])
-            return w_raw
+        grids = (make_grid(0, BANKS0, BANK // P), make_grid(1, 1, BANK // P), make_grid(2, 1, 1))
 
         def quantise_weights(level, w_raw):
             passes = CHANNELS[level] // K_PASS
@@ -117,16 +134,56 @@ def tile_objectboxdetect_k_kernel(tc, x0, x1, x2, W0, b0, W1, b1, W2, b2, out):
                 )
             return w_codes, w_scales
 
-        def finish(level, acc, per_part, grid, stores):
+        def quantise_small(level, raw):
+            passes = CHANNELS[level] // K_PASS
+            cells = SIDE[level] * SIDE[level]
+            grouped = keep.tile([P, passes, B, cells, PACK], BF16, name="grouped%d" % level, align_bytes=64)
+            for n in range(B):
+                copy = nc.vector.tensor_copy if n == 0 else nc.scalar.copy
+                for g in range(passes):
+                    regroup(copy, grouped[:, g, n, :, :], raw[:, n, g, :, :])
+            codes = keep.tile([P, passes, B * cells], U32, name="codes%d" % level, align_bytes=64)
+            scales = keep.tile([P, passes, B * cells], U8, name="scales%d" % level, align_bytes=64)
+            nc.vector.quantize_mx(
+                out=codes[:].rearrange("p g w -> p (g w)").bitcast(FP8X4),
+                scales=scales[:].rearrange("p g w -> p (g w)"),
+                in_=grouped[:].rearrange("p g n w j -> p (g n w j)"),
+            )
+            return codes, scales
+
+        def multiply_small(level, w_mx, x_mx):
+            passes = CHANNELS[level] // K_PASS
+            cells = SIDE[level] * SIDE[level]
+            acc = acc_pool.tile([P, B * cells], F32, name="acc", tag="acc")
+            for g in range(passes):
+                nc.tensor.matmul_mx(
+                    out=acc[:],
+                    lhsT=w_mx[0][:, g, :].bitcast(FP8X4), lhsT_scale=w_mx[1][:, g, :],
+                    rhs=x_mx[0][:, g, :].bitcast(FP8X4), rhs_scale=x_mx[1][:, g, :],
+                    start=(g == 0), stop=(g == passes - 1),
+                )
+            half = P // B
+            first = FIRST_ROW[level]
+            targets = [(out[n, first : first + cells, :], slice(n * half, (n + 1) * half)) for n in range(B)]
+            return (level, acc, B * cells // P, grids[level][:, 0, :, :], targets)
+
+        stores = []
+
+        def squash(group):
+            level, acc, per_part, grid, targets = group
             y = work.tile([P, per_part, P], F32, name="y", tag="y")
             nc.scalar.activation(
-                out=y[:], in_=acc.rearrange("o (p t) -> o t p", t=per_part), func=ACT.Sigmoid,
+                out=y[:], in_=acc[:].rearrange("o (p t) -> o t p", t=per_part), func=ACT.Sigmoid,
                 bias=bias_sb[level][:, 0:1], scale=1.0,
             )
             turned = turn_pool.tile([P, per_part, NO], F32, name="turned", tag="turn")
             for t in range(per_part):
                 nc.tensor.transpose(turned[:, t, :], y[:, t, :], ident[:])
-            res = work.tile([P, per_part, NO], F32, name="res", tag="res")
+            return (level, turned, per_part, grid, targets)
+
+        def decode(group):
+            level, turned, per_part, grid, targets = group
+            res = keep.tile([P, per_part, NO], F32, name="res%d" % len(stores))
             nc.vector.tensor_copy(out=res[:], in_=turned[:])
             stride, power = STRIDE[level], POWER[level]
             sq = work.tile([P, per_part, 4], F32, name="sq", tag="sq")
@@ -143,50 +200,15 @@ def tile_objectboxdetect_k_kernel(tc, x0, x1, x2, W0, b0, W1, b1, W2, b2, out):
                 out=res[:, :, 2:4], in0=total[:], scalar1=4.0 * stride * power, scalar2=-stride,
                 op0=ALU.mult, op1=ALU.add,
             )
-            for rows, parts in stores:
-                nc.sync.dma_start(out=rows.rearrange("(p t) o -> p t o", t=per_part), in_=res[parts, :, :])
+            for rows, parts in targets:
+                stores.append((rows.rearrange("(p t) o -> p t o", t=per_part), res[parts, :, :]))
 
-        def small_level(level, x):
-            passes = CHANNELS[level] // K_PASS
-            cells = SIDE[level] * SIDE[level]
-            w_raw = load_weights(level)
-            raw = keep.tile([P, B, passes, PACK, cells], BF16, name="raw%d" % level)
-            nc.sync.dma_start(
-                out=raw[:].rearrange("p n g j w -> p (n g) (j w)"),
-                in_=x.rearrange("n (g p j) r c -> p (n g) (j r c)", p=P, j=PACK),
-            )
-            w_codes, w_scales = quantise_weights(level, w_raw)
-            grouped = keep.tile([P, passes, B, cells, PACK], BF16, name="grouped%d" % level, align_bytes=64)
-            for n in range(B):
-                copy = nc.vector.tensor_copy if n == 0 else nc.scalar.copy
-                for g in range(passes):
-                    regroup(copy, grouped[:, g, n, :, :], raw[:, n, g, :, :])
-            codes = keep.tile([P, passes, B * cells], U32, name="codes%d" % level, align_bytes=64)
-            scales = keep.tile([P, passes, B * cells], U8, name="scales%d" % level, align_bytes=64)
-            nc.vector.quantize_mx(
-                out=codes[:].rearrange("p g w -> p (g w)").bitcast(FP8X4),
-                scales=scales[:].rearrange("p g w -> p (g w)"),
-                in_=grouped[:].rearrange("p g n w j -> p (g n w j)"),
-            )
-            acc = acc_pool.tile([P, B * cells], F32, name="acc", tag="acc")
-            for g in range(passes):
-                nc.tensor.matmul_mx(
-                    out=acc[:],
-                    lhsT=w_codes[:, g, :].bitcast(FP8X4), lhsT_scale=w_scales[:, g, :],
-                    rhs=codes[:, g, :].bitcast(FP8X4), rhs_scale=scales[:, g, :],
-                    start=(g == 0), stop=(g == passes - 1),
-                )
-            half = P // B
-            first = FIRST_ROW[level]
-            finish(
-                level, acc[:], B * cells // P, grids[level][:, 0, :, :],
-                [(out[n, first : first + cells, :], slice(n * half, (n + 1) * half)) for n in range(B)],
-            )
-
-        small_level(2, x2)
-        small_level(1, x1)
-
-        w_codes0, w_scales0 = quantise_weights(0, load_weights(0))
+        w_mx2 = quantise_weights(2, w_raw2)
+        w_mx1 = quantise_weights(1, w_raw1)
+        x_mx2 = quantise_small(2, raw2)
+        x_mx1 = quantise_small(1, raw1)
+        w_codes0, w_scales0 = quantise_weights(0, w_raw0)
+        complete = [multiply_small(2, w_mx2, x_mx2), multiply_small(1, w_mx1, x_mx1)]
 
         def load_and_regroup(n, c):
             raw = raw_pool.tile([P, PACK, CELLS0], BF16, name="raw")
@@ -201,29 +223,38 @@ def tile_objectboxdetect_k_kernel(tc, x0, x1, x2, W0, b0, W1, b1, W2, b2, out):
 
         chunks = [(n, c) for n in range(B) for c in range(PASSES0)]
         grouped_next = load_and_regroup(*chunks[0])
-        acc = None
-        for i, (n, c) in enumerate(chunks):
-            grouped = grouped_next
-            if i + 1 < len(chunks):
-                grouped_next = load_and_regroup(*chunks[i + 1])
-            codes = work.tile([P, CELLS0], U32, name="codes", tag="codes", align_bytes=64)
-            scales = work.tile([P, CELLS0], U8, name="scales", tag="scales", align_bytes=64)
-            nc.vector.quantize_mx(
-                out=codes[:].bitcast(FP8X4), scales=scales[:], in_=grouped[:].rearrange("p w j -> p (w j)"),
-            )
-            if c == 0:
-                acc = [acc_pool.tile([P, BANK], F32, name="acc%d" % h, tag="acc") for h in range(CELLS0 // BANK)]
-            for h in range(CELLS0 // BANK):
-                cols = slice(h * BANK, (h + 1) * BANK)
-                nc.tensor.matmul_mx(
-                    out=acc[h][:],
-                    lhsT=w_codes0[:, c, :].bitcast(FP8X4), lhsT_scale=w_scales0[:, c, :],
-                    rhs=codes[:, cols].bitcast(FP8X4), rhs_scale=scales[:, cols],
-                    start=(c == 0), stop=(c == PASSES0 - 1),
+        acc = []
+        squashed = []
+        for step in range(len(chunks) + 2):
+            to_decode, to_squash, complete = squashed, complete, []
+            if step < len(chunks):
+                n, c = chunks[step]
+                grouped = grouped_next
+                if step + 1 < len(chunks):
+                    grouped_next = load_and_regroup(*chunks[step + 1])
+                codes = work.tile([P, CELLS0], U32, name="codes", tag="codes", align_bytes=64)
+                scales = work.tile([P, CELLS0], U8, name="scales", tag="scales", align_bytes=64)
+                nc.vector.quantize_mx(
+                    out=codes[:].bitcast(FP8X4), scales=scales[:], in_=grouped[:].rearrange("p w j -> p (w j)"),
                 )
-            if c == PASSES0 - 1:
-                for h in range(CELLS0 // BANK):
-                    finish(
-                        0, acc[h][:], BANK // P, grids[0][:, h, :, :],
-                        [(out[n, h * BANK : (h + 1) * BANK, :], slice(0, P))],
+                if c == 0:
+                    acc = [acc_pool.tile([P, BANK], F32, name="acc%d" % h, tag="acc") for h in range(BANKS0)]
+                for h in range(BANKS0):
+                    cols = slice(h * BANK, (h + 1) * BANK)
+                    nc.tensor.matmul_mx(
+                        out=acc[h][:],
+                        lhsT=w_codes0[:, c, :].bitcast(FP8X4), lhsT_scale=w_scales0[:, c, :],
+                        rhs=codes[:, cols].bitcast(FP8X4), rhs_scale=scales[:, cols],
+                        start=(c == 0), stop=(c == PASSES0 - 1),
                     )
+                if c == PASSES0 - 1:
+                    complete = [
+                        (0, acc[h], BANK // P, grids[0][:, h, :, :], [(out[n, h * BANK : (h + 1) * BANK, :], slice(0, P))])
+                        for h in range(BANKS0)
+                    ]
+            for group in to_decode:
+                decode(group)
+            squashed = [squash(group) for group in to_squash]
+
+        for rows, res in stores:
+            nc.sync.dma_start(out=rows, in_=res)

@@ -19,6 +19,8 @@ BANK = 512
 B = 2
 NO = 128
 RUN = 4
+BANK_PASSES = 2
+QUANT_PASSES = 8
 
 CHANNELS = (8192, 512, 1024)
 SIDE = (32, 16, 8)
@@ -30,7 +32,7 @@ FIRST_ROW = (0, 1024, 1280)
 CELLS0 = SIDE[0] * SIDE[0]
 BANKS0 = CELLS0 // BANK
 PASSES0 = CHANNELS[0] // K_PASS
-VECTOR_CELLS = 512
+VECTOR_CELLS = 496
 
 FLOPS = 2 * NO * B * (8192 * 32 * 32 + 512 * 16 * 16 + 1024 * 8 * 8)
 
@@ -117,19 +119,25 @@ def tile_objectboxdetect_k_kernel(tc, x0, x1, x2, W0, b0, W1, b1, W2, b2, out):
             w_scales = keep.tile([P, passes, NO], U8, name="w_scales%d" % level, align_bytes=64)
             w_words = w_raw[:].bitcast(F32)
             words = K_PASS // 2
-            for g0 in range(0, passes, 2):
-                count = min(2, passes - g0)
-                planes = turn_pool.tile([P, count, 2, NO], F32, name="planes", tag="turn")
-                for j in range(count):
-                    for u in range(2):
-                        first = (g0 + j) * words + u
-                        nc.tensor.transpose(planes[:, j, u, :], w_words[:, first : (g0 + j + 1) * words : 2], ident[:])
-                w_grouped = work.tile([P, count, NO, PACK], BF16, name="w_grouped", tag="w_grouped", align_bytes=64)
-                copy = nc.vector.tensor_copy if (g0 // 2) % 2 == 0 else nc.scalar.copy
-                copy(out=w_grouped[:].bitcast(F32), in_=planes[:].rearrange("p j u o -> p j o u"))
+            for q0 in range(0, passes, QUANT_PASSES):
+                q_count = min(QUANT_PASSES, passes - q0)
+                w_grouped = work.tile([P, q_count, NO, PACK], BF16, name="w_grouped", tag="w_grouped", align_bytes=64)
+                for g0 in range(q0, q0 + q_count, BANK_PASSES):
+                    count = min(BANK_PASSES, passes - g0)
+                    planes = turn_pool.tile([P, count, 2, NO], F32, name="planes", tag="turn")
+                    for j in range(count):
+                        for u in range(2):
+                            first = (g0 + j) * words + u
+                            nc.tensor.transpose(
+                                planes[:, j, u, :], w_words[:, first : (g0 + j + 1) * words : 2], ident[:]
+                            )
+                    nc.scalar.copy(
+                        out=w_grouped[:, g0 - q0 : g0 - q0 + count, :, :].bitcast(F32),
+                        in_=planes[:].rearrange("p j u o -> p j o u"),
+                    )
                 nc.vector.quantize_mx(
-                    out=w_codes[:, g0 : g0 + count, :].rearrange("p g o -> p (g o)").bitcast(FP8X4),
-                    scales=w_scales[:, g0 : g0 + count, :].rearrange("p g o -> p (g o)"),
+                    out=w_codes[:, q0 : q0 + q_count, :].rearrange("p g o -> p (g o)").bitcast(FP8X4),
+                    scales=w_scales[:, q0 : q0 + q_count, :].rearrange("p g o -> p (g o)"),
                     in_=w_grouped[:].rearrange("p g o t -> p (g o t)"),
                 )
             return w_codes, w_scales
@@ -164,51 +172,61 @@ def tile_objectboxdetect_k_kernel(tc, x0, x1, x2, W0, b0, W1, b1, W2, b2, out):
                 )
             half = P // B
             first = FIRST_ROW[level]
-            targets = [(out[n, first : first + cells, :], slice(n * half, (n + 1) * half)) for n in range(B)]
-            return (level, acc, B * cells // P, grids[level][:, 0, :, :], targets)
+            targets = [
+                (out[n, first : first + cells, :].rearrange("(h p t) o -> p h (t o)", h=1, p=half), slice(n * half, (n + 1) * half))
+                for n in range(B)
+            ]
+            return (level, [acc], B * cells // P, targets)
 
         stores = []
 
         def squash(group):
-            level, acc, per_part, grid, targets = group
-            y = work.tile([P, per_part, P], F32, name="y", tag="y")
-            nc.scalar.activation(
-                out=y[:], in_=acc[:].rearrange("o (p t) -> o t p", t=per_part), func=ACT.Sigmoid,
-                bias=bias_sb[level][:, 0:1], scale=1.0,
-            )
-            turned = turn_pool.tile([P, per_part, NO], F32, name="turned", tag="turn")
-            for t in range(per_part):
-                nc.tensor.transpose(turned[:, t, :], y[:, t, :], ident[:])
-            return (level, turned, per_part, grid, targets)
+            level, banks, per_part, targets = group
+            turned_banks = []
+            for acc in banks:
+                y = work.tile([P, per_part, P], F32, name="y", tag="y")
+                nc.scalar.activation(
+                    out=y[:], in_=acc[:].rearrange("o (p t) -> o t p", t=per_part), func=ACT.Sigmoid,
+                    bias=bias_sb[level][:, 0:1], scale=1.0,
+                )
+                turned = turn_pool.tile([P, per_part, NO], F32, name="turned", tag="turn")
+                for t in range(per_part):
+                    nc.tensor.transpose(turned[:, t, :], y[:, t, :], ident[:])
+                turned_banks.append(turned)
+            return (level, turned_banks, per_part, targets)
 
         def decode(group):
-            level, turned, per_part, grid, targets = group
-            res = keep.tile([P, per_part, NO], F32, name="res%d" % len(stores))
-            nc.vector.tensor_copy(out=res[:], in_=turned[:])
+            level, banks, per_part, targets = group
+            res = keep.tile([P, len(banks), per_part, NO], F32, name="res%d" % len(stores))
+            for h, turned in enumerate(banks):
+                copy = nc.vector.tensor_copy if h % 2 == 0 else nc.scalar.copy
+                copy(out=res[:, h, :, :], in_=turned[:])
             stride, power = STRIDE[level], POWER[level]
-            sq = work.tile([P, per_part, 4], F32, name="sq", tag="sq")
-            nc.vector.tensor_tensor(out=sq[:], in0=res[:, :, 0:4], in1=res[:, :, 0:4], op=ALU.mult)
-            diff = work.tile([P, per_part, 2], F32, name="diff", tag="diff")
+            cells = len(banks) * per_part
+            box = res[:].rearrange("p h t o -> p (h t) o")
+            sq = work.tile([P, cells, 4], F32, name="sq", tag="sq")
+            nc.vector.tensor_tensor(out=sq[:], in0=box[:, :, 0:4], in1=box[:, :, 0:4], op=ALU.mult)
+            diff = work.tile([P, cells, 2], F32, name="diff", tag="diff")
             nc.vector.tensor_tensor(out=diff[:], in0=sq[:, :, 2:4], in1=sq[:, :, 0:2], op=ALU.subtract)
-            total = work.tile([P, per_part, 2], F32, name="total", tag="total")
+            total = work.tile([P, cells, 2], F32, name="total", tag="total")
             nc.vector.tensor_tensor(out=total[:], in0=sq[:, :, 2:4], in1=sq[:, :, 0:2], op=ALU.add)
             nc.vector.scalar_tensor_tensor(
-                out=res[:, :, 0:2], in0=diff[:], scalar=2.0 * stride * power, in1=grid,
-                op0=ALU.mult, op1=ALU.add,
+                out=box[:, :, 0:2], in0=diff[:], scalar=2.0 * stride * power,
+                in1=grids[level][:].rearrange("p h t a -> p (h t) a"), op0=ALU.mult, op1=ALU.add,
             )
             nc.vector.tensor_scalar(
-                out=res[:, :, 2:4], in0=total[:], scalar1=4.0 * stride * power, scalar2=-stride,
+                out=box[:, :, 2:4], in0=total[:], scalar1=4.0 * stride * power, scalar2=-stride,
                 op0=ALU.mult, op1=ALU.add,
             )
             for rows, parts in targets:
-                stores.append((rows.rearrange("(p t) o -> p t o", t=per_part), res[parts, :, :]))
+                stores.append((rows, res[parts, :, :, :].rearrange("p h t o -> p h (t o)")))
 
         w_mx2 = quantise_weights(2, w_raw2)
         w_mx1 = quantise_weights(1, w_raw1)
         x_mx2 = quantise_small(2, raw2)
         x_mx1 = quantise_small(1, raw1)
         w_codes0, w_scales0 = quantise_weights(0, w_raw0)
-        complete = [multiply_small(2, w_mx2, x_mx2), multiply_small(1, w_mx1, x_mx1)]
+        small = [multiply_small(2, w_mx2, x_mx2), multiply_small(1, w_mx1, x_mx1)]
 
         def load_and_regroup(n, c):
             raw = raw_pool.tile([P, PACK, CELLS0], BF16, name="raw")
@@ -222,39 +240,41 @@ def tile_objectboxdetect_k_kernel(tc, x0, x1, x2, W0, b0, W1, b1, W2, b2, out):
             return grouped
 
         chunks = [(n, c) for n in range(B) for c in range(PASSES0)]
-        grouped_next = load_and_regroup(*chunks[0])
+        last = len(chunks) - 1
+        images = []
         acc = []
-        squashed = []
-        for step in range(len(chunks) + 2):
-            to_decode, to_squash, complete = squashed, complete, []
-            if step < len(chunks):
-                n, c = chunks[step]
-                grouped = grouped_next
-                if step + 1 < len(chunks):
-                    grouped_next = load_and_regroup(*chunks[step + 1])
-                codes = work.tile([P, CELLS0], U32, name="codes", tag="codes", align_bytes=64)
-                scales = work.tile([P, CELLS0], U8, name="scales", tag="scales", align_bytes=64)
-                nc.vector.quantize_mx(
-                    out=codes[:].bitcast(FP8X4), scales=scales[:], in_=grouped[:].rearrange("p w j -> p (w j)"),
+        first_turned = None
+        grouped_next = load_and_regroup(*chunks[0])
+        for step, (n, c) in enumerate(chunks):
+            grouped = grouped_next
+            if step < last:
+                grouped_next = load_and_regroup(*chunks[step + 1])
+            if step == last:
+                first_turned = squash(images[0])
+            codes = work.tile([P, CELLS0], U32, name="codes", tag="codes", align_bytes=64)
+            scales = work.tile([P, CELLS0], U8, name="scales", tag="scales", align_bytes=64)
+            nc.vector.quantize_mx(
+                out=codes[:].bitcast(FP8X4), scales=scales[:], in_=grouped[:].rearrange("p w j -> p (w j)"),
+            )
+            if c == 0:
+                acc = [acc_pool.tile([P, BANK], F32, name="acc%d" % h, tag="acc") for h in range(BANKS0)]
+                rows = out[n, 0:CELLS0, :].rearrange("(h p t) o -> p h (t o)", h=BANKS0, p=P)
+                images.append((0, acc, BANK // P, [(rows, slice(0, P))]))
+            for h in range(BANKS0):
+                cols = slice(h * BANK, (h + 1) * BANK)
+                nc.tensor.matmul_mx(
+                    out=acc[h][:],
+                    lhsT=w_codes0[:, c, :].bitcast(FP8X4), lhsT_scale=w_scales0[:, c, :],
+                    rhs=codes[:, cols].bitcast(FP8X4), rhs_scale=scales[:, cols],
+                    start=(c == 0), stop=(c == PASSES0 - 1),
                 )
-                if c == 0:
-                    acc = [acc_pool.tile([P, BANK], F32, name="acc%d" % h, tag="acc") for h in range(BANKS0)]
-                for h in range(BANKS0):
-                    cols = slice(h * BANK, (h + 1) * BANK)
-                    nc.tensor.matmul_mx(
-                        out=acc[h][:],
-                        lhsT=w_codes0[:, c, :].bitcast(FP8X4), lhsT_scale=w_scales0[:, c, :],
-                        rhs=codes[:, cols].bitcast(FP8X4), rhs_scale=scales[:, cols],
-                        start=(c == 0), stop=(c == PASSES0 - 1),
-                    )
-                if c == PASSES0 - 1:
-                    complete = [
-                        (0, acc[h], BANK // P, grids[0][:, h, :, :], [(out[n, h * BANK : (h + 1) * BANK, :], slice(0, P))])
-                        for h in range(BANKS0)
-                    ]
-            for group in to_decode:
-                decode(group)
-            squashed = [squash(group) for group in to_squash]
+            if step == 0:
+                small = [squash(group) for group in small]
+            if step == 1:
+                for group in small:
+                    decode(group)
+        decode(first_turned)
+        decode(squash(images[1]))
 
         for rows, res in stores:
             nc.sync.dma_start(out=rows, in_=res)

@@ -18,7 +18,7 @@ K_PASS = P * PACK
 BANK = 512
 B = 2
 NO = 128
-RUN = 4
+RUN = 8
 BANK_PASSES = 2
 QUANT_PASSES = 8
 

@@ -33,6 +33,8 @@ CELLS0 = SIDE[0] * SIDE[0]
 BANKS0 = CELLS0 // BANK
 PASSES0 = CHANNELS[0] // K_PASS
 VECTOR_CELLS = 496
+TENSOR_CELLS = 208
+TENSOR_PIECE = 104
 
 FLOPS = 2 * NO * B * (8192 * 32 * 32 + 512 * 16 * 16 + 1024 * 8 * 8)
 
@@ -87,6 +89,8 @@ def tile_objectboxdetect_k_kernel(tc, x0, x1, x2, W0, b0, W1, b1, W2, b2, out):
 
         ident = keep.tile([P, P], F32, name="ident")
         make_identity(nc, ident[:])
+        ident_bf = keep.tile([P, P], BF16, name="ident_bf")
+        make_identity(nc, ident_bf[:])
 
         warm = keep.tile([P, 1], F32, name="warm")
         nc.vector.memset(warm[:], 0.0)
@@ -235,8 +239,24 @@ def tile_objectboxdetect_k_kernel(tc, x0, x1, x2, W0, b0, W1, b1, W2, b2, out):
                 in_=x0[n, c * K_PASS : (c + 1) * K_PASS, :, :].rearrange("(p j) r c -> p j (r c)", j=PACK),
             )
             grouped = work.tile([P, CELLS0, PACK], BF16, name="grouped", tag="grouped", align_bytes=64)
+            scalar_end = CELLS0 - TENSOR_CELLS if c % 2 == 0 else CELLS0
+            passed = None
+            if scalar_end < CELLS0:
+                passed = turn_pool.tile([P, TENSOR_CELLS, PACK], BF16, name="passed", tag="turn")
+                for first in range(0, TENSOR_CELLS, TENSOR_PIECE):
+                    nc.tensor.matmul(
+                        out=passed[:, first : first + TENSOR_PIECE, :].rearrange("p w j -> p (w j)"),
+                        lhsT=ident_bf[:],
+                        rhs=raw[:, :, scalar_end + first : scalar_end + first + TENSOR_PIECE].rearrange("p j w -> p w j"),
+                        start=True, stop=True,
+                    )
             regroup(nc.vector.tensor_copy, grouped[:, :VECTOR_CELLS, :], raw[:, :, :VECTOR_CELLS])
-            regroup(nc.scalar.copy, grouped[:, VECTOR_CELLS:, :], raw[:, :, VECTOR_CELLS:])
+            regroup(nc.scalar.copy, grouped[:, VECTOR_CELLS:scalar_end, :], raw[:, :, VECTOR_CELLS:scalar_end])
+            if passed is not None:
+                nc.scalar.copy(
+                    out=grouped[:, scalar_end:, :].rearrange("p w j -> p (w j)"),
+                    in_=passed[:].rearrange("p w j -> p (w j)"),
+                )
             return grouped
 
         chunks = [(n, c) for n in range(B) for c in range(PASSES0)]

@@ -33,6 +33,7 @@ CELLS0 = SIDE[0] * SIDE[0]
 BANKS0 = CELLS0 // BANK
 PASSES0 = CHANNELS[0] // K_PASS
 VECTOR_CELLS = 496
+VECTOR_CELLS_HELPED = 448
 TENSOR_CELLS = 208
 TENSOR_PIECE = 104
 
@@ -232,16 +233,15 @@ def tile_objectboxdetect_k_kernel(tc, x0, x1, x2, W0, b0, W1, b1, W2, b2, out):
         w_codes0, w_scales0 = quantise_weights(0, w_raw0)
         small = [multiply_small(2, w_mx2, x_mx2), multiply_small(1, w_mx1, x_mx1)]
 
-        def load_and_regroup(n, c):
+        def load(n, c):
             raw = raw_pool.tile([P, PACK, CELLS0], BF16, name="raw")
             nc.sync.dma_start(
                 out=raw[:],
                 in_=x0[n, c * K_PASS : (c + 1) * K_PASS, :, :].rearrange("(p j) r c -> p j (r c)", j=PACK),
             )
-            grouped = work.tile([P, CELLS0, PACK], BF16, name="grouped", tag="grouped", align_bytes=64)
-            scalar_end = CELLS0 - TENSOR_CELLS if c % 2 == 0 else CELLS0
+            scalar_end = CELLS0 - TENSOR_CELLS
             passed = None
-            if scalar_end < CELLS0:
+            if c % 2 == 0:
                 passed = turn_pool.tile([P, TENSOR_CELLS, PACK], BF16, name="passed", tag="turn")
                 for first in range(0, TENSOR_CELLS, TENSOR_PIECE):
                     nc.tensor.matmul(
@@ -250,8 +250,14 @@ def tile_objectboxdetect_k_kernel(tc, x0, x1, x2, W0, b0, W1, b1, W2, b2, out):
                         rhs=raw[:, :, scalar_end + first : scalar_end + first + TENSOR_PIECE].rearrange("p j w -> p w j"),
                         start=True, stop=True,
                     )
-            regroup(nc.vector.tensor_copy, grouped[:, :VECTOR_CELLS, :], raw[:, :, :VECTOR_CELLS])
-            regroup(nc.scalar.copy, grouped[:, VECTOR_CELLS:scalar_end, :], raw[:, :, VECTOR_CELLS:scalar_end])
+            return raw, passed
+
+        def regroup_chunk(raw, passed):
+            grouped = work.tile([P, CELLS0, PACK], BF16, name="grouped", tag="grouped", align_bytes=64)
+            vector_end = VECTOR_CELLS if passed is None else VECTOR_CELLS_HELPED
+            scalar_end = CELLS0 if passed is None else CELLS0 - TENSOR_CELLS
+            regroup(nc.vector.tensor_copy, grouped[:, :vector_end, :], raw[:, :, :vector_end])
+            regroup(nc.scalar.copy, grouped[:, vector_end:scalar_end, :], raw[:, :, vector_end:scalar_end])
             if passed is not None:
                 nc.scalar.copy(
                     out=grouped[:, scalar_end:, :].rearrange("p w j -> p (w j)"),
@@ -264,11 +270,15 @@ def tile_objectboxdetect_k_kernel(tc, x0, x1, x2, W0, b0, W1, b1, W2, b2, out):
         images = []
         acc = []
         first_turned = None
-        grouped_next = load_and_regroup(*chunks[0])
+        grouped_next = regroup_chunk(*load(*chunks[0]))
+        loaded_next = load(*chunks[1])
         for step, (n, c) in enumerate(chunks):
             grouped = grouped_next
+            loaded = loaded_next
+            if step + 2 <= last:
+                loaded_next = load(*chunks[step + 2])
             if step < last:
-                grouped_next = load_and_regroup(*chunks[step + 1])
+                grouped_next = regroup_chunk(*loaded)
             if step == last:
                 first_turned = squash(images[0])
             codes = work.tile([P, CELLS0], U32, name="codes", tag="codes", align_bytes=64)

@@ -245,9 +245,9 @@ def tile_objectboxdetect_k_kernel(tc, x0, x1, x2, W0, b0, W1, b1, W2, b2, out):
                 passed = turn_pool.tile([P, TENSOR_CELLS, PACK], BF16, name="passed", tag="turn")
                 for first in range(0, TENSOR_CELLS, TENSOR_PIECE):
                     nc.tensor.matmul(
-                        out=passed[:, first : first + TENSOR_PIECE, :].rearrange("p w j -> p (w j)"),
+                        out=passed[:, first : first + TENSOR_PIECE, :].rearrange("p (c i) j -> p c j i", i=RUN),
                         lhsT=ident_bf[:],
-                        rhs=raw[:, :, scalar_end + first : scalar_end + first + TENSOR_PIECE].rearrange("p j w -> p w j"),
+                        rhs=raw[:, :, scalar_end + first : scalar_end + first + TENSOR_PIECE].rearrange("p j (c i) -> p c j i", i=RUN),
                         start=True, stop=True,
                     )
             return raw, passed

from contextlib import ExitStack

import concourse.mybir as mybir
from concourse.masks import make_identity

BF16 = mybir.dt.bfloat16
F32 = mybir.dt.float32
I32 = mybir.dt.int32
U32 = mybir.dt.uint32
U8 = mybir.dt.uint8
FP8X4 = mybir.dt.float8_e4m3fn_x4
ACT = mybir.ActivationFunctionType
ALU = mybir.AluOpType

P = 128
PACK = 4
K_PASS = P * PACK
BANK = 512
B = 2
NO = 128
RUN = 8
BANK_PASSES = 2
QUANT_PASSES = 8

CHANNELS = (8192, 512, 1024)
SIDE = (32, 16, 8)
SIDE_BITS = (5, 4, 3)
STRIDE = (8.0, 16.0, 32.0)
POWER = (1.0, 2.0, 4.0)
FIRST_ROW = (0, 1024, 1280)

CELLS0 = SIDE[0] * SIDE[0]
BANKS0 = CELLS0 // BANK
PASSES0 = CHANNELS[0] // K_PASS
VECTOR_CELLS = 496
VECTOR_CELLS_HELPED = 448
TENSOR_CELLS = 208
TENSOR_PIECE = 104

FLOPS = 2 * NO * B * (8192 * 32 * 32 + 512 * 16 * 16 + 1024 * 8 * 8)


def regroup(copy, grouped, raw):
    copy(
        out=grouped.rearrange("p (c i) j -> p c j i", i=RUN),
        in_=raw.rearrange("p j (c i) -> p c j i", i=RUN),
    )


def tile_objectboxdetect_k_kernel(tc, x0, x1, x2, W0, b0, W1, b1, W2, b2, out):
    nc = tc.nc
    features = (x0, x1, x2)
    weights = (W0, W1, W2)
    biases = (b0, b1, b2)

    with ExitStack() as ctx:
        ctx.enter_context(tc.manual_schedule())
        keep = ctx.enter_context(tc.tile_pool(name="keep", bufs=1))
        raw_pool = ctx.enter_context(tc.tile_pool(name="raw", bufs=8))
        work = ctx.enter_context(tc.tile_pool(name="work", bufs=3))
        acc_pool = ctx.enter_context(tc.psum_pool(name="acc", bufs=4))
        turn_pool = ctx.enter_context(tc.psum_pool(name="turn", bufs=4))

        bias_sb = []
        for level in range(3):
            bias = keep.tile([P, 1], BF16, name="bias%d" % level)
            nc.scalar.dma_start(out=bias[:], in_=biases[level].rearrange("(o one) -> o one", one=1))
            bias_sb.append(bias)

        def load_weights(level):
            w_raw = keep.tile([P, CHANNELS[level]], BF16, name="w_raw%d" % level)
            piece = min(CHANNELS[level], 4 * K_PASS)
            for first in range(0, CHANNELS[level], piece):
                nc.sync.dma_start(out=w_raw[:, first : first + piece], in_=weights[level][:, first : first + piece])
            return w_raw

        def load_small(level):
            raw = keep.tile(
                [P, B, CHANNELS[level] // K_PASS, PACK, SIDE[level] * SIDE[level]], BF16, name="raw%d" % level
            )
            nc.sync.dma_start(
                out=raw[:].rearrange("p n g j w -> p (n g) (j w)"),
                in_=features[level].rearrange("n (g p j) r c -> p (n g) (j r c)", p=P, j=PACK),
            )
            return raw

        w_raw2, w_raw1 = load_weights(2), load_weights(1)
        raw2, raw1 = load_small(2), load_small(1)
        w_raw0 = load_weights(0)

        ident = keep.tile([P, P], F32, name="ident")
        make_identity(nc, ident[:])
        ident_bf = keep.tile([P, P], BF16, name="ident_bf")
        make_identity(nc, ident_bf[:])

        warm = keep.tile([P, 1], F32, name="warm")
        nc.vector.memset(warm[:], 0.0)
        nc.scalar.activation(out=warm[:], in_=warm[:], func=ACT.Sigmoid)

        def make_grid(level, banks, per_part):
            side = SIDE[level]
            cell = keep.tile([P, banks, per_part], I32, name="cell%d" % level)
            nc.gpsimd.iota(cell[:], pattern=[[BANK, banks], [1, per_part]], base=0, channel_multiplier=per_part)
            col = keep.tile([P, banks, per_part], I32, name="col%d" % level)
            nc.vector.tensor_scalar(out=col[:], in0=cell[:], scalar1=side - 1, scalar2=None, op0=ALU.bitwise_and)
            row = keep.tile([P, banks, per_part], I32, name="row%d" % level)
            nc.vector.tensor_scalar(
                out=row[:], in0=cell[:], scalar1=side * side - 1, scalar2=SIDE_BITS[level],
                op0=ALU.bitwise_and, op1=ALU.logical_shift_right,
            )
            grid = keep.tile([P, banks, per_part, 2], F32, name="grid%d" % level)
            for axis, index in enumerate((col, row)):
                nc.vector.tensor_scalar(
                    out=grid[:, :, :, axis], in0=index[:], scalar1=0.5, scalar2=STRIDE[level],
                    op0=ALU.add, op1=ALU.mult,
                )
            return grid

        grids = (make_grid(0, BANKS0, BANK // P), make_grid(1, 1, BANK // P), make_grid(2, 1, 1))

        def quantise_weights(level, w_raw):
            passes = CHANNELS[level] // K_PASS
            w_codes = keep.tile([P, passes, NO], U32, name="w_codes%d" % level, align_bytes=64)
            w_scales = keep.tile([P, passes, NO], U8, name="w_scales%d" % level, align_bytes=64)
            w_words = w_raw[:].bitcast(F32)
            words = K_PASS // 2
            for q0 in range(0, passes, QUANT_PASSES):
                q_count = min(QUANT_PASSES, passes - q0)
                w_grouped = work.tile([P, q_count, NO, PACK], BF16, name="w_grouped", tag="w_grouped", align_bytes=64)
                for g0 in range(q0, q0 + q_count, BANK_PASSES):
                    count = min(BANK_PASSES, passes - g0)
                    planes = turn_pool.tile([P, count, 2, NO], F32, name="planes", tag="turn")
                    for j in range(count):
                        for u in range(2):
                            first = (g0 + j) * words + u
                            nc.tensor.transpose(
                                planes[:, j, u, :], w_words[:, first : (g0 + j + 1) * words : 2], ident[:]
                            )
                    nc.scalar.copy(
                        out=w_grouped[:, g0 - q0 : g0 - q0 + count, :, :].bitcast(F32),
                        in_=planes[:].rearrange("p j u o -> p j o u"),
                    )
                nc.vector.quantize_mx(
                    out=w_codes[:, q0 : q0 + q_count, :].rearrange("p g o -> p (g o)").bitcast(FP8X4),
                    scales=w_scales[:, q0 : q0 + q_count, :].rearrange("p g o -> p (g o)"),
                    in_=w_grouped[:].rearrange("p g o t -> p (g o t)"),
                )
            return w_codes, w_scales

        def quantise_small(level, raw):
            passes = CHANNELS[level] // K_PASS
            cells = SIDE[level] * SIDE[level]
            grouped = keep.tile([P, passes, B, cells, PACK], BF16, name="grouped%d" % level, align_bytes=64)
            for n in range(B):
                copy = nc.vector.tensor_copy if n == 0 else nc.scalar.copy
                for g in range(passes):
                    regroup(copy, grouped[:, g, n, :, :], raw[:, n, g, :, :])
            codes = keep.tile([P, passes, B * cells], U32, name="codes%d" % level, align_bytes=64)
            scales = keep.tile([P, passes, B * cells], U8, name="scales%d" % level, align_bytes=64)
            nc.vector.quantize_mx(
                out=codes[:].rearrange("p g w -> p (g w)").bitcast(FP8X4),
                scales=scales[:].rearrange("p g w -> p (g w)"),
                in_=grouped[:].rearrange("p g n w j -> p (g n w j)"),
            )
            return codes, scales

        def multiply_small(level, w_mx, x_mx):
            passes = CHANNELS[level] // K_PASS
            cells = SIDE[level] * SIDE[level]
            acc = acc_pool.tile([P, B * cells], F32, name="acc", tag="acc")
            for g in range(passes):
                nc.tensor.matmul_mx(
                    out=acc[:],
                    lhsT=w_mx[0][:, g, :].bitcast(FP8X4), lhsT_scale=w_mx[1][:, g, :],
                    rhs=x_mx[0][:, g, :].bitcast(FP8X4), rhs_scale=x_mx[1][:, g, :],
                    start=(g == 0), stop=(g == passes - 1),
                )
            half = P // B
            first = FIRST_ROW[level]
            targets = [
                (out[n, first : first + cells, :].rearrange("(h p t) o -> p h (t o)", h=1, p=half), slice(n * half, (n + 1) * half))
                for n in range(B)
            ]
            return (level, [acc], B * cells // P, targets)

        stores = []

        def squash(group):
            level, banks, per_part, targets = group
            turned_banks = []
            for acc in banks:
                y = work.tile([P, per_part, P], F32, name="y", tag="y")
                nc.scalar.activation(
                    out=y[:], in_=acc[:].rearrange("o (p t) -> o t p", t=per_part), func=ACT.Sigmoid,
                    bias=bias_sb[level][:, 0:1], scale=1.0,
                )
                turned = turn_pool.tile([P, per_part, NO], F32, name="turned", tag="turn")
                for t in range(per_part):
                    nc.tensor.transpose(turned[:, t, :], y[:, t, :], ident[:])
                turned_banks.append(turned)
            return (level, turned_banks, per_part, targets)

        def decode(group):
            level, banks, per_part, targets = group
            res = keep.tile([P, len(banks), per_part, NO], F32, name="res%d" % len(stores))
            for h, turned in enumerate(banks):
                copy = nc.vector.tensor_copy if h % 2 == 0 else nc.scalar.copy
                copy(out=res[:, h, :, :], in_=turned[:])
            stride, power = STRIDE[level], POWER[level]
            cells = len(banks) * per_part
            box = res[:].rearrange("p h t o -> p (h t) o")
            sq = work.tile([P, cells, 4], F32, name="sq", tag="sq")
            nc.vector.tensor_tensor(out=sq[:], in0=box[:, :, 0:4], in1=box[:, :, 0:4], op=ALU.mult)
            diff = work.tile([P, cells, 2], F32, name="diff", tag="diff")
            nc.vector.tensor_tensor(out=diff[:], in0=sq[:, :, 2:4], in1=sq[:, :, 0:2], op=ALU.subtract)
            total = work.tile([P, cells, 2], F32, name="total", tag="total")
            nc.vector.tensor_tensor(out=total[:], in0=sq[:, :, 2:4], in1=sq[:, :, 0:2], op=ALU.add)
            nc.vector.scalar_tensor_tensor(
                out=box[:, :, 0:2], in0=diff[:], scalar=2.0 * stride * power,
                in1=grids[level][:].rearrange("p h t a -> p (h t) a"), op0=ALU.mult, op1=ALU.add,
            )
            nc.vector.tensor_scalar(
                out=box[:, :, 2:4], in0=total[:], scalar1=4.0 * stride * power, scalar2=-stride,
                op0=ALU.mult, op1=ALU.add,
            )
            for rows, parts in targets:
                stores.append((rows, res[parts, :, :, :].rearrange("p h t o -> p h (t o)")))

        w_mx2 = quantise_weights(2, w_raw2)
        w_mx1 = quantise_weights(1, w_raw1)
        x_mx2 = quantise_small(2, raw2)
        x_mx1 = quantise_small(1, raw1)
        w_codes0, w_scales0 = quantise_weights(0, w_raw0)
        small = [multiply_small(2, w_mx2, x_mx2), multiply_small(1, w_mx1, x_mx1)]

        def load(n, c):
            raw = raw_pool.tile([P, PACK, CELLS0], BF16, name="raw")
            nc.sync.dma_start(
                out=raw[:],
                in_=x0[n, c * K_PASS : (c + 1) * K_PASS, :, :].rearrange("(p j) r c -> p j (r c)", j=PACK),
            )
            scalar_end = CELLS0 - TENSOR_CELLS
            passed = None
            if c % 2 == 0:
                passed = turn_pool.tile([P, TENSOR_CELLS, PACK], BF16, name="passed", tag="turn")
                for first in range(0, TENSOR_CELLS, TENSOR_PIECE):
                    nc.tensor.matmul(
                        out=passed[:, first : first + TENSOR_PIECE, :].rearrange("p (c i) j -> p c j i", i=RUN),
                        lhsT=ident_bf[:],
                        rhs=raw[:, :, scalar_end + first : scalar_end + first + TENSOR_PIECE].rearrange("p j (c i) -> p c j i", i=RUN),
                        start=True, stop=True,
                    )
            return raw, passed

        def regroup_chunk(raw, passed):
            grouped = work.tile([P, CELLS0, PACK], BF16, name="grouped", tag="grouped", align_bytes=64)
            vector_end = VECTOR_CELLS if passed is None else VECTOR_CELLS_HELPED
            scalar_end = CELLS0 if passed is None else CELLS0 - TENSOR_CELLS
            regroup(nc.vector.tensor_copy, grouped[:, :vector_end, :], raw[:, :, :vector_end])
            regroup(nc.scalar.copy, grouped[:, vector_end:scalar_end, :], raw[:, :, vector_end:scalar_end])
            if passed is not None:
                nc.scalar.copy(
                    out=grouped[:, scalar_end:, :].rearrange("p w j -> p (w j)"),
                    in_=passed[:].rearrange("p w j -> p (w j)"),
                )
            return grouped

        chunks = [(n, c) for n in range(B) for c in range(PASSES0)]
        last = len(chunks) - 1
        images = []
        acc = []
        first_turned = None
        grouped_next = regroup_chunk(*load(*chunks[0]))
        loaded_next = load(*chunks[1])
        for step, (n, c) in enumerate(chunks):
            grouped = grouped_next
            loaded = loaded_next
            if step + 2 <= last:
                loaded_next = load(*chunks[step + 2])
            if step < last:
                grouped_next = regroup_chunk(*loaded)
            if step == last:
                first_turned = squash(images[0])
            codes = work.tile([P, CELLS0], U32, name="codes", tag="codes", align_bytes=64)
            scales = work.tile([P, CELLS0], U8, name="scales", tag="scales", align_bytes=64)
            nc.vector.quantize_mx(
                out=codes[:].bitcast(FP8X4), scales=scales[:], in_=grouped[:].rearrange("p w j -> p (w j)"),
            )
            if c == 0:
                acc = [acc_pool.tile([P, BANK], F32, name="acc%d" % h, tag="acc") for h in range(BANKS0)]
                rows = out[n, 0:CELLS0, :].rearrange("(h p t) o -> p h (t o)", h=BANKS0, p=P)
                images.append((0, acc, BANK // P, [(rows, slice(0, P))]))
            for h in range(BANKS0):
                cols = slice(h * BANK, (h + 1) * BANK)
                nc.tensor.matmul_mx(
                    out=acc[h][:],
                    lhsT=w_codes0[:, c, :].bitcast(FP8X4), lhsT_scale=w_scales0[:, c, :],
                    rhs=codes[:, cols].bitcast(FP8X4), rhs_scale=scales[:, cols],
                    start=(c == 0), stop=(c == PASSES0 - 1),
                )
            if step == 0:
                small = [squash(group) for group in small]
            if step == 1:
                for group in small:
                    decode(group)
        decode(first_turned)
        decode(squash(images[1]))

        for rows, res in stores:
            nc.sync.dma_start(out=rows, in_=res)
